import numpy as np
import ml_dtypes

BF16 = ml_dtypes.bfloat16


def bf(x):
    return np.asarray(x, np.float32).astype(BF16)


def f32(x):
    return np.asarray(x, np.float32)


def f64(x):
    return np.asarray(x).astype(np.float64)


def striped(idx):
    return np.tile(idx.reshape(-1, 16).T, (8, 1))


S, K, HID, M, N = 512, 128, 256, 512, 1024


def setup_inputs():
    return {
        "table": bf(np.random.standard_normal((K, S))),
        "w": bf(np.random.standard_normal((K, M)) / np.sqrt(K)),
        "b1": f32(0.2 * np.random.standard_normal((M, 1))),
        "w2s": bf(0.5 * np.random.standard_normal((HID, K)) / np.sqrt(HID)),
        "b2s": f32(0.2 * np.random.standard_normal((K, 1))),
        "w2t": bf(np.random.standard_normal((HID, K)) / np.sqrt(HID)),
        "b2t": f32(0.2 * np.random.standard_normal((K, 1))),
        "zb": f32(np.random.standard_normal((K, N))),
        "offs": striped(np.random.permutation(np.tile(np.arange(S), 2))[:N]),
    }


def reference(table, w, b1, w2s, b2s, w2t, b2t, zb, offs):
    idx = offs[:16].T.reshape(-1)
    h = np.maximum(f64(w).T @ f64(table)[:, idx] + f64(b1), 0.0)
    s = f64(w2s).T @ h[:HID] + f64(b2s)
    t = f64(w2t).T @ h[HID:] + f64(b2t)
    return f64(zb) * np.exp(s) + t

@@ -1,0 +1,89 @@
+import concourse.mybir as mybir
+
+BF16, F32, U16 = mybir.dt.bfloat16, mybir.dt.float32, mybir.dt.uint16
+ADD, MAX, MULT = mybir.AluOpType.add, mybir.AluOpType.max, mybir.AluOpType.mult
+RELU, EXP = mybir.ActivationFunctionType.Relu, mybir.ActivationFunctionType.Exp
+
+P = 128
+STORE = 512
+HIDDEN = 512
+N = 1024
+PIECE = 512
+PIECES = N // PIECE
+BLOCKS = HIDDEN // P
+NET_BLOCKS = BLOCKS // 2
+LIST_COLS = PIECE // 16
+
+FLOPS = 2 * P * HIDDEN * N + 2 * HIDDEN * P * N
+
+
+def tile_affinecoupling_kernel(tc, table, w, b1, w2s, b2s, w2t, b2t, zb, offs, out):
+    nc = tc.nc
+    with (
+        tc.tile_pool(name="held", bufs=1) as held,
+        tc.tile_pool(name="work", bufs=2) as work,
+        tc.psum_pool(name="hidden_psum", bufs=4) as hidden_psum,
+        tc.psum_pool(name="net_psum", bufs=2) as net_psum,
+    ):
+        offsets = held.tile([P, N // 16], U16, name="offsets")
+        nc.sync.dma_start(offsets[:], offs)
+        table_sb = held.tile([P, STORE], BF16, name="table_sb")
+        nc.sync.dma_start(table_sb[:], table)
+        w_sb = held.tile([P, HIDDEN], BF16, name="w_sb")
+        nc.scalar.dma_start(w_sb[:], w)
+
+        b1_sb = held.tile([P, BLOCKS, 1], F32, name="b1_sb")
+        b2s_sb = held.tile([P, 1], F32, name="b2s_sb")
+        b2t_sb = held.tile([P, 1], F32, name="b2t_sb")
+        with nc.allow_non_contiguous_dma(reason="biases: one float32 a partition"):
+            nc.sync.dma_start(b1_sb[:], b1.rearrange("(b p) o -> p b o", p=P))
+            nc.scalar.dma_start(b2s_sb[:], b2s)
+            nc.scalar.dma_start(b2t_sb[:], b2t)
+
+        w2s_sb = held.tile([P, NET_BLOCKS, P], BF16, name="w2s_sb")
+        nc.scalar.dma_start(w2s_sb[:], w2s.rearrange("(b p) c -> p b c", p=P))
+        w2t_sb = held.tile([P, NET_BLOCKS, P], BF16, name="w2t_sb")
+        nc.scalar.dma_start(w2t_sb[:], w2t.rearrange("(b p) c -> p b c", p=P))
+        zb_sb = held.tile([P, N], F32, name="zb_sb")
+        nc.sync.dma_start(zb_sb[:], zb)
+
+        hidden = {}
+        for piece in range(PIECES):
+            piece_offsets = offsets[:, piece * LIST_COLS : (piece + 1) * LIST_COLS]
+            for block in range(BLOCKS):
+                h_ps = hidden_psum.tile([P, PIECE], F32, name="h_ps")
+                nc.tensor.matmul(
+                    h_ps[:],
+                    w_sb[:, block * P : (block + 1) * P],
+                    table_sb[:].indirect(piece_offsets),
+                    start=True,
+                    stop=True,
+                )
+                h_sb = held.tile([P, PIECE], BF16, name=f"h_sb_{piece}_{block}")
+                if block % 2 == 0:
+                    nc.scalar.activation(h_sb[:], h_ps[:], RELU, bias=b1_sb[:, block, :])
+                else:
+                    nc.vector.tensor_scalar(h_sb[:], h_ps[:], b1_sb[:, block, :], 0.0, ADD, MAX)
+                hidden[piece, block] = h_sb
+
+        for piece in range(PIECES):
+            columns = slice(piece * PIECE, (piece + 1) * PIECE)
+            s_ps = net_psum.tile([P, PIECE], F32, name="s_ps")
+            for b in range(NET_BLOCKS):
+                nc.tensor.matmul(
+                    s_ps[:], w2s_sb[:, b, :], hidden[piece, b][:],
+                    start=(b == 0), stop=(b == NET_BLOCKS - 1),
+                )
+            t_ps = net_psum.tile([P, PIECE], F32, name="t_ps")
+            for b in range(NET_BLOCKS):
+                nc.tensor.matmul(
+                    t_ps[:], w2t_sb[:, b, :], hidden[piece, NET_BLOCKS + b][:],
+                    start=(b == 0), stop=(b == NET_BLOCKS - 1),
+                )
+            scale = work.tile([P, PIECE], F32, name="scale")
+            nc.scalar.activation(scale[:], s_ps[:], EXP, bias=b2s_sb[:])
+            scaled = work.tile([P, PIECE], F32, name="scaled")
+            nc.vector.tensor_tensor(scaled[:], scale[:], zb_sb[:, columns], MULT)
+            result = work.tile([P, PIECE], F32, name="result")
+            nc.vector.scalar_tensor_tensor(result[:], t_ps[:], b2t_sb[:], scaled[:], ADD, ADD)
+            nc.sync.dma_start(out[:, columns], result[:])

@@ -13,6 +13,7 @@ PIECES = N // PIECE
 BLOCKS = HIDDEN // P
 NET_BLOCKS = BLOCKS // 2
 LIST_COLS = PIECE // 16
+WARM_MATMULS = 5
 
 FLOPS = 2 * P * HIDDEN * N + 2 * HIDDEN * P * N
 
@@ -32,20 +33,28 @@ def tile_affinecoupling_kernel(tc, table, w, b1, w2s, b2s, w2t, b2t, zb, offs, o
         w_sb = held.tile([P, HIDDEN], BF16, name="w_sb")
         nc.scalar.dma_start(w_sb[:], w)
 
+        zeros = held.tile([P, PIECE], BF16, name="zeros")
+        nc.vector.memset(zeros[:], 0.0)
+        warm_ps = hidden_psum.tile([P, PIECE], F32, name="warm_ps", tag="h_ps")
+        for i in range(WARM_MATMULS):
+            nc.tensor.matmul(warm_ps[:], zeros[:, 0:P], zeros[:], start=True, stop=True)
+        table_warm = held.tile([P, 1], F32, name="table_warm")
+        nc.scalar.activation(table_warm[:], zeros[:, 0:1], EXP)
+
         b1_sb = held.tile([P, BLOCKS, 1], F32, name="b1_sb")
         b2s_sb = held.tile([P, 1], F32, name="b2s_sb")
         b2t_sb = held.tile([P, 1], F32, name="b2t_sb")
         with nc.allow_non_contiguous_dma(reason="biases: one float32 a partition"):
             nc.sync.dma_start(b1_sb[:], b1.rearrange("(b p) o -> p b o", p=P))
-            nc.scalar.dma_start(b2s_sb[:], b2s)
-            nc.scalar.dma_start(b2t_sb[:], b2t)
+            nc.sync.dma_start(b2s_sb[:], b2s)
+            nc.sync.dma_start(b2t_sb[:], b2t)
 
         w2s_sb = held.tile([P, NET_BLOCKS, P], BF16, name="w2s_sb")
-        nc.scalar.dma_start(w2s_sb[:], w2s.rearrange("(b p) c -> p b c", p=P))
+        nc.gpsimd.dma_start(w2s_sb[:], w2s.rearrange("(b p) c -> p b c", p=P))
         w2t_sb = held.tile([P, NET_BLOCKS, P], BF16, name="w2t_sb")
-        nc.scalar.dma_start(w2t_sb[:], w2t.rearrange("(b p) c -> p b c", p=P))
+        nc.gpsimd.dma_start(w2t_sb[:], w2t.rearrange("(b p) c -> p b c", p=P))
         zb_sb = held.tile([P, N], F32, name="zb_sb")
-        nc.sync.dma_start(zb_sb[:], zb)
+        nc.gpsimd.dma_start(zb_sb[:], zb)
 
         hidden = {}
         for piece in range(PIECES):

@@ -57,42 +57,48 @@ def tile_affinecoupling_kernel(tc, table, w, b1, w2s, b2s, w2t, b2t, zb, offs, o
         nc.gpsimd.dma_start(zb_sb[:], zb)
 
         hidden = {}
-        for piece in range(PIECES):
-            piece_offsets = offsets[:, piece * LIST_COLS : (piece + 1) * LIST_COLS]
-            for block in range(BLOCKS):
-                h_ps = hidden_psum.tile([P, PIECE], F32, name="h_ps")
-                nc.tensor.matmul(
-                    h_ps[:],
-                    w_sb[:, block * P : (block + 1) * P],
-                    table_sb[:].indirect(piece_offsets),
-                    start=True,
-                    stop=True,
-                )
-                h_sb = held.tile([P, PIECE], BF16, name=f"h_sb_{piece}_{block}")
-                if block % 2 == 0:
-                    nc.scalar.activation(h_sb[:], h_ps[:], RELU, bias=b1_sb[:, block, :])
-                else:
-                    nc.vector.tensor_scalar(h_sb[:], h_ps[:], b1_sb[:, block, :], 0.0, ADD, MAX)
-                hidden[piece, block] = h_sb
+        for net in range(2):
+            for piece in range(PIECES):
+                piece_offsets = offsets[:, piece * LIST_COLS : (piece + 1) * LIST_COLS]
+                for block in range(net * NET_BLOCKS, (net + 1) * NET_BLOCKS):
+                    h_ps = hidden_psum.tile([P, PIECE], F32, name="h_ps")
+                    nc.tensor.matmul(
+                        h_ps[:],
+                        w_sb[:, block * P : (block + 1) * P],
+                        table_sb[:].indirect(piece_offsets),
+                        start=True,
+                        stop=True,
+                    )
+                    h_sb = held.tile([P, PIECE], BF16, name=f"h_sb_{piece}_{block}")
+                    if block % 2 == 0:
+                        nc.scalar.activation(h_sb[:], h_ps[:], RELU, bias=b1_sb[:, block, :])
+                    else:
+                        nc.vector.tensor_scalar(h_sb[:], h_ps[:], b1_sb[:, block, :], 0.0, ADD, MAX)
+                    hidden[piece, block] = h_sb
 
+        s_banks, t_banks = [], []
         for piece in range(PIECES):
-            columns = slice(piece * PIECE, (piece + 1) * PIECE)
             s_ps = net_psum.tile([P, PIECE], F32, name="s_ps")
             for b in range(NET_BLOCKS):
                 nc.tensor.matmul(
                     s_ps[:], w2s_sb[:, b, :], hidden[piece, b][:],
                     start=(b == 0), stop=(b == NET_BLOCKS - 1),
                 )
+            s_banks.append(s_ps)
+        for piece in range(PIECES):
             t_ps = net_psum.tile([P, PIECE], F32, name="t_ps")
             for b in range(NET_BLOCKS):
                 nc.tensor.matmul(
                     t_ps[:], w2t_sb[:, b, :], hidden[piece, NET_BLOCKS + b][:],
                     start=(b == 0), stop=(b == NET_BLOCKS - 1),
                 )
+            t_banks.append(t_ps)
+        for piece in range(PIECES):
+            columns = slice(piece * PIECE, (piece + 1) * PIECE)
             scale = work.tile([P, PIECE], F32, name="scale")
-            nc.scalar.activation(scale[:], s_ps[:], EXP, bias=b2s_sb[:])
+            nc.scalar.activation(scale[:], s_banks[piece][:], EXP, bias=b2s_sb[:])
             scaled = work.tile([P, PIECE], F32, name="scaled")
             nc.vector.tensor_tensor(scaled[:], scale[:], zb_sb[:, columns], MULT)
             result = work.tile([P, PIECE], F32, name="result")
-            nc.vector.scalar_tensor_tensor(result[:], t_ps[:], b2t_sb[:], scaled[:], ADD, ADD)
+            nc.vector.scalar_tensor_tensor(result[:], t_banks[piece][:], b2t_sb[:], scaled[:], ADD, ADD)
             nc.sync.dma_start(out[:, columns], result[:])

@@ -13,7 +13,10 @@ PIECES = N // PIECE
 BLOCKS = HIDDEN // P
 NET_BLOCKS = BLOCKS // 2
 LIST_COLS = PIECE // 16
-WARM_MATMULS = 5
+CHUNK = 256
+CHUNKS = N // CHUNK
+BANKS = 8
+WARM_MATMULS = 16
 
 FLOPS = 2 * P * HIDDEN * N + 2 * HIDDEN * P * N
 
@@ -22,10 +25,12 @@ def tile_affinecoupling_kernel(tc, table, w, b1, w2s, b2s, w2t, b2t, zb, offs, o
     nc = tc.nc
     with (
         tc.tile_pool(name="held", bufs=1) as held,
-        tc.tile_pool(name="work", bufs=2) as work,
-        tc.psum_pool(name="hidden_psum", bufs=4) as hidden_psum,
-        tc.psum_pool(name="net_psum", bufs=2) as net_psum,
+        tc.tile_pool(name="work", bufs=CHUNKS) as work,
+        tc.psum_pool(name="psum", bufs=BANKS) as psum,
     ):
+        zeros = held.tile([P, P], BF16, name="zeros")
+        nc.vector.memset(zeros[:], 0.0)
+
         offsets = held.tile([P, N // 16], U16, name="offsets")
         nc.sync.dma_start(offsets[:], offs)
         table_sb = held.tile([P, STORE], BF16, name="table_sb")
@@ -33,11 +38,9 @@ def tile_affinecoupling_kernel(tc, table, w, b1, w2s, b2s, w2t, b2t, zb, offs, o
         w_sb = held.tile([P, HIDDEN], BF16, name="w_sb")
         nc.scalar.dma_start(w_sb[:], w)
 
-        zeros = held.tile([P, PIECE], BF16, name="zeros")
-        nc.vector.memset(zeros[:], 0.0)
-        warm_ps = hidden_psum.tile([P, PIECE], F32, name="warm_ps", tag="h_ps")
+        warm_ps = psum.tile([P, P], F32, name="warm_ps", tag="bank")
         for i in range(WARM_MATMULS):
-            nc.tensor.matmul(warm_ps[:], zeros[:, 0:P], zeros[:], start=True, stop=True)
+            nc.tensor.matmul(warm_ps[:], zeros[:], zeros[:], start=True, stop=True)
         table_warm = held.tile([P, 1], F32, name="table_warm")
         nc.scalar.activation(table_warm[:], zeros[:, 0:1], EXP)
 
@@ -50,18 +53,18 @@ def tile_affinecoupling_kernel(tc, table, w, b1, w2s, b2s, w2t, b2t, zb, offs, o
             nc.sync.dma_start(b2t_sb[:], b2t)
 
         w2s_sb = held.tile([P, NET_BLOCKS, P], BF16, name="w2s_sb")
-        nc.gpsimd.dma_start(w2s_sb[:], w2s.rearrange("(b p) c -> p b c", p=P))
+        nc.scalar.dma_start(w2s_sb[:], w2s.rearrange("(b p) c -> p b c", p=P))
         w2t_sb = held.tile([P, NET_BLOCKS, P], BF16, name="w2t_sb")
-        nc.gpsimd.dma_start(w2t_sb[:], w2t.rearrange("(b p) c -> p b c", p=P))
+        nc.scalar.dma_start(w2t_sb[:], w2t.rearrange("(b p) c -> p b c", p=P))
         zb_sb = held.tile([P, N], F32, name="zb_sb")
-        nc.gpsimd.dma_start(zb_sb[:], zb)
+        nc.sync.dma_start(zb_sb[:], zb)
 
-        hidden = {}
+        hidden = [held.tile([P, N], BF16, name=f"hidden{block}") for block in range(BLOCKS)]
         for net in range(2):
             for piece in range(PIECES):
                 piece_offsets = offsets[:, piece * LIST_COLS : (piece + 1) * LIST_COLS]
                 for block in range(net * NET_BLOCKS, (net + 1) * NET_BLOCKS):
-                    h_ps = hidden_psum.tile([P, PIECE], F32, name="h_ps")
+                    h_ps = psum.tile([P, PIECE], F32, name="h_ps", tag="bank")
                     nc.tensor.matmul(
                         h_ps[:],
                         w_sb[:, block * P : (block + 1) * P],
@@ -69,36 +72,35 @@ def tile_affinecoupling_kernel(tc, table, w, b1, w2s, b2s, w2t, b2t, zb, offs, o
                         start=True,
                         stop=True,
                     )
-                    h_sb = held.tile([P, PIECE], BF16, name=f"h_sb_{piece}_{block}")
+                    h_sb = hidden[block][:, piece * PIECE : (piece + 1) * PIECE]
                     if block % 2 == 0:
-                        nc.scalar.activation(h_sb[:], h_ps[:], RELU, bias=b1_sb[:, block, :])
+                        nc.scalar.activation(h_sb, h_ps[:], RELU, bias=b1_sb[:, block, :])
                     else:
-                        nc.vector.tensor_scalar(h_sb[:], h_ps[:], b1_sb[:, block, :], 0.0, ADD, MAX)
-                    hidden[piece, block] = h_sb
+                        nc.vector.tensor_scalar(h_sb, h_ps[:], b1_sb[:, block, :], 0.0, ADD, MAX)
 
         s_banks, t_banks = [], []
-        for piece in range(PIECES):
-            s_ps = net_psum.tile([P, PIECE], F32, name="s_ps")
-            for b in range(NET_BLOCKS):
-                nc.tensor.matmul(
-                    s_ps[:], w2s_sb[:, b, :], hidden[piece, b][:],
-                    start=(b == 0), stop=(b == NET_BLOCKS - 1),
-                )
-            s_banks.append(s_ps)
-        for piece in range(PIECES):
-            t_ps = net_psum.tile([P, PIECE], F32, name="t_ps")
-            for b in range(NET_BLOCKS):
-                nc.tensor.matmul(
-                    t_ps[:], w2t_sb[:, b, :], hidden[piece, NET_BLOCKS + b][:],
-                    start=(b == 0), stop=(b == NET_BLOCKS - 1),
-                )
-            t_banks.append(t_ps)
-        for piece in range(PIECES):
-            columns = slice(piece * PIECE, (piece + 1) * PIECE)
-            scale = work.tile([P, PIECE], F32, name="scale")
-            nc.scalar.activation(scale[:], s_banks[piece][:], EXP, bias=b2s_sb[:])
-            scaled = work.tile([P, PIECE], F32, name="scaled")
-            nc.vector.tensor_tensor(scaled[:], scale[:], zb_sb[:, columns], MULT)
-            result = work.tile([P, PIECE], F32, name="result")
-            nc.vector.scalar_tensor_tensor(result[:], t_banks[piece][:], b2t_sb[:], scaled[:], ADD, ADD)
-            nc.sync.dma_start(out[:, columns], result[:])
+        for banks, weights, first_block in ((s_banks, w2s_sb, 0), (t_banks, w2t_sb, NET_BLOCKS)):
+            for chunk in range(CHUNKS):
+                net_ps = psum.tile([P, CHUNK], F32, name="net_ps", tag="bank")
+                for b in range(NET_BLOCKS):
+                    nc.tensor.matmul(
+                        net_ps[:],
+                        weights[:, b, :],
+                        hidden[first_block + b][:, chunk * CHUNK : (chunk + 1) * CHUNK],
+                        start=(b == 0),
+                        stop=(b == NET_BLOCKS - 1),
+                    )
+                banks.append(net_ps)
+
+        products = []
+        for chunk in range(CHUNKS):
+            scale = work.tile([P, CHUNK], F32, name="scale")
+            nc.scalar.activation(scale[:], s_banks[chunk][:], EXP, bias=b2s_sb[:])
+            scaled = work.tile([P, CHUNK], F32, name="scaled")
+            nc.vector.tensor_tensor(scaled[:], scale[:], zb_sb[:, chunk * CHUNK : (chunk + 1) * CHUNK], MULT)
+            products.append(scaled)
+        for chunk in range(CHUNKS):
+            result = work.tile([P, CHUNK], F32, name="result")
+            nc.vector.scalar_tensor_tensor(result[:], t_banks[chunk][:], b2t_sb[:], products[chunk][:], ADD, ADD)
+            store_queue = nc.sync if chunk % 2 == 0 else nc.scalar
+            store_queue.dma_start(out[:, chunk * CHUNK : (chunk + 1) * CHUNK], result[:])

@@ -8,13 +8,13 @@ P = 128
 STORE = 512
 HIDDEN = 512
 N = 1024
-PIECE = 512
-PIECES = N // PIECE
 BLOCKS = HIDDEN // P
 NET_BLOCKS = BLOCKS // 2
-LIST_COLS = PIECE // 16
+S_NET, T_NET = 0, 1
+HALF = 512
 CHUNK = 256
 CHUNKS = N // CHUNK
+S_GROUP = 64
 BANKS = 8
 WARM_MATMULS = 16
 
@@ -60,47 +60,54 @@ def tile_affinecoupling_kernel(tc, table, w, b1, w2s, b2s, w2t, b2t, zb, offs, o
         nc.sync.dma_start(zb_sb[:], zb)
 
         hidden = [held.tile([P, N], BF16, name=f"hidden{block}") for block in range(BLOCKS)]
-        for net in range(2):
-            for piece in range(PIECES):
-                piece_offsets = offsets[:, piece * LIST_COLS : (piece + 1) * LIST_COLS]
-                for block in range(net * NET_BLOCKS, (net + 1) * NET_BLOCKS):
-                    h_ps = psum.tile([P, PIECE], F32, name="h_ps", tag="bank")
-                    nc.tensor.matmul(
-                        h_ps[:],
-                        w_sb[:, block * P : (block + 1) * P],
-                        table_sb[:].indirect(piece_offsets),
-                        start=True,
-                        stop=True,
-                    )
-                    h_sb = hidden[block][:, piece * PIECE : (piece + 1) * PIECE]
-                    if block % 2 == 0:
-                        nc.scalar.activation(h_sb, h_ps[:], RELU, bias=b1_sb[:, block, :])
-                    else:
-                        nc.vector.tensor_scalar(h_sb, h_ps[:], b1_sb[:, block, :], 0.0, ADD, MAX)
 
-        s_banks, t_banks = [], []
-        for banks, weights, first_block in ((s_banks, w2s_sb, 0), (t_banks, w2t_sb, NET_BLOCKS)):
-            for chunk in range(CHUNKS):
-                net_ps = psum.tile([P, CHUNK], F32, name="net_ps", tag="bank")
+        def first_layer(net, first, width):
+            picked = table_sb[:].indirect(offsets[:, first // 16 : (first + width) // 16])
+            for block in range(net * NET_BLOCKS, (net + 1) * NET_BLOCKS):
+                h_ps = psum.tile([P, width], F32, name="h_ps", tag="bank")
+                nc.tensor.matmul(h_ps[:], w_sb[:, block * P : (block + 1) * P], picked, start=True, stop=True)
+                h_sb = hidden[block][:, first : first + width]
+                if block % 2 == 0:
+                    nc.scalar.activation(h_sb, h_ps[:], RELU, bias=b1_sb[:, block, :])
+                else:
+                    nc.vector.tensor_scalar(h_sb, h_ps[:], b1_sb[:, block, :], 0.0, ADD, MAX)
+
+        def second_layer(net, weights, chunk, width):
+            net_ps = psum.tile([P, CHUNK], F32, name="net_ps", tag="bank")
+            for group in range(0, CHUNK, width):
+                first = chunk * CHUNK + group
                 for b in range(NET_BLOCKS):
                     nc.tensor.matmul(
-                        net_ps[:],
+                        net_ps[:, group : group + width],
                         weights[:, b, :],
-                        hidden[first_block + b][:, chunk * CHUNK : (chunk + 1) * CHUNK],
+                        hidden[net * NET_BLOCKS + b][:, first : first + width],
                         start=(b == 0),
                         stop=(b == NET_BLOCKS - 1),
                     )
-                banks.append(net_ps)
+            return net_ps
 
-        products = []
-        for chunk in range(CHUNKS):
+        def scaled_zb(chunk, s_ps):
             scale = work.tile([P, CHUNK], F32, name="scale")
-            nc.scalar.activation(scale[:], s_banks[chunk][:], EXP, bias=b2s_sb[:])
+            nc.scalar.activation(scale[:], s_ps[:], EXP, bias=b2s_sb[:])
             scaled = work.tile([P, CHUNK], F32, name="scaled")
             nc.vector.tensor_tensor(scaled[:], scale[:], zb_sb[:, chunk * CHUNK : (chunk + 1) * CHUNK], MULT)
-            products.append(scaled)
-        for chunk in range(CHUNKS):
+            return scaled
+
+        def finish(chunk, t_ps, scaled):
             result = work.tile([P, CHUNK], F32, name="result")
-            nc.vector.scalar_tensor_tensor(result[:], t_banks[chunk][:], b2t_sb[:], products[chunk][:], ADD, ADD)
+            nc.vector.scalar_tensor_tensor(result[:], t_ps[:], b2t_sb[:], scaled[:], ADD, ADD)
             store_queue = nc.sync if chunk % 2 == 0 else nc.scalar
             store_queue.dma_start(out[:, chunk * CHUNK : (chunk + 1) * CHUNK], result[:])
+
+
+        first_layer(S_NET, 0, HALF)
+        first_layer(S_NET, HALF, HALF)
+        first_layer(T_NET, 0, HALF)
+
+        products = [scaled_zb(chunk, second_layer(S_NET, w2s_sb, chunk, S_GROUP)) for chunk in range(CHUNKS)]
+
+        for chunk in range(HALF // CHUNK, CHUNKS):
+            first_layer(T_NET, chunk * CHUNK, CHUNK)
+
+        for chunk in range(CHUNKS):
+            finish(chunk, second_layer(T_NET, w2t_sb, chunk, CHUNK), products[chunk])

@@ -16,7 +16,6 @@ CHUNK = 256
 CHUNKS = N // CHUNK
 S_GROUP = 64
 BANKS = 8
-WARM_MATMULS = 16
 
 FLOPS = 2 * P * HIDDEN * N + 2 * HIDDEN * P * N
 
@@ -28,7 +27,7 @@ def tile_affinecoupling_kernel(tc, table, w, b1, w2s, b2s, w2t, b2t, zb, offs, o
         tc.tile_pool(name="work", bufs=CHUNKS) as work,
         tc.psum_pool(name="psum", bufs=BANKS) as psum,
     ):
-        zeros = held.tile([P, P], BF16, name="zeros")
+        zeros = held.tile([P, 1], F32, name="zeros")
         nc.vector.memset(zeros[:], 0.0)
 
         offsets = held.tile([P, N // 16], U16, name="offsets")
@@ -38,11 +37,8 @@ def tile_affinecoupling_kernel(tc, table, w, b1, w2s, b2s, w2t, b2t, zb, offs, o
         w_sb = held.tile([P, HIDDEN], BF16, name="w_sb")
         nc.scalar.dma_start(w_sb[:], w)
 
-        warm_ps = psum.tile([P, P], F32, name="warm_ps", tag="bank")
-        for i in range(WARM_MATMULS):
-            nc.tensor.matmul(warm_ps[:], zeros[:], zeros[:], start=True, stop=True)
         table_warm = held.tile([P, 1], F32, name="table_warm")
-        nc.scalar.activation(table_warm[:], zeros[:, 0:1], EXP)
+        nc.scalar.activation(table_warm[:], zeros[:], EXP)
 
         b1_sb = held.tile([P, BLOCKS, 1], F32, name="b1_sb")
         b2s_sb = held.tile([P, 1], F32, name="b2s_sb")

@@ -24,21 +24,22 @@ def tile_affinecoupling_kernel(tc, table, w, b1, w2s, b2s, w2t, b2t, zb, offs, o
     nc = tc.nc
     with (
         tc.tile_pool(name="held", bufs=1) as held,
-        tc.tile_pool(name="work", bufs=CHUNKS) as work,
+        tc.tile_pool(name="work", bufs=CHUNKS + 1) as work,
         tc.psum_pool(name="psum", bufs=BANKS) as psum,
     ):
         zeros = held.tile([P, 1], F32, name="zeros")
         nc.vector.memset(zeros[:], 0.0)
 
-        offsets = held.tile([P, N // 16], U16, name="offsets")
-        nc.sync.dma_start(offsets[:], offs)
         table_sb = held.tile([P, STORE], BF16, name="table_sb")
         nc.sync.dma_start(table_sb[:], table)
+        offsets = held.tile([P, N // 16], U16, name="offsets")
+        nc.sync.dma_start(offsets[:], offs)
         w_sb = held.tile([P, HIDDEN], BF16, name="w_sb")
-        nc.scalar.dma_start(w_sb[:], w)
+        nc.scalar.dma_start(w_sb[:, : HIDDEN // 2], w[:, : HIDDEN // 2])
 
         table_warm = held.tile([P, 1], F32, name="table_warm")
         nc.scalar.activation(table_warm[:], zeros[:], EXP)
+        nc.scalar.dma_start(w_sb[:, HIDDEN // 2 :], w[:, HIDDEN // 2 :])
 
         b1_sb = held.tile([P, BLOCKS, 1], F32, name="b1_sb")
         b2s_sb = held.tile([P, 1], F32, name="b2s_sb")
@@ -68,15 +69,14 @@ def tile_affinecoupling_kernel(tc, table, w, b1, w2s, b2s, w2t, b2t, zb, offs, o
                 else:
                     nc.vector.tensor_scalar(h_sb, h_ps[:], b1_sb[:, block, :], 0.0, ADD, MAX)
 
-        def second_layer(net, weights, chunk, width):
-            net_ps = psum.tile([P, CHUNK], F32, name="net_ps", tag="bank")
-            for group in range(0, CHUNK, width):
-                first = chunk * CHUNK + group
+        def second_layer(net, weights, first, width, group):
+            net_ps = psum.tile([P, width], F32, name="net_ps", tag="bank")
+            for col in range(0, width, group):
                 for b in range(NET_BLOCKS):
                     nc.tensor.matmul(
-                        net_ps[:, group : group + width],
+                        net_ps[:, col : col + group],
                         weights[:, b, :],
-                        hidden[net * NET_BLOCKS + b][:, first : first + width],
+                        hidden[net * NET_BLOCKS + b][:, first + col : first + col + group],
                         start=(b == 0),
                         stop=(b == NET_BLOCKS - 1),
                     )
@@ -89,21 +89,26 @@ def tile_affinecoupling_kernel(tc, table, w, b1, w2s, b2s, w2t, b2t, zb, offs, o
             nc.vector.tensor_tensor(scaled[:], scale[:], zb_sb[:, chunk * CHUNK : (chunk + 1) * CHUNK], MULT)
             return scaled
 
-        def finish(chunk, t_ps, scaled):
-            result = work.tile([P, CHUNK], F32, name="result")
-            nc.vector.scalar_tensor_tensor(result[:], t_ps[:], b2t_sb[:], scaled[:], ADD, ADD)
-            store_queue = nc.sync if chunk % 2 == 0 else nc.scalar
-            store_queue.dma_start(out[:, chunk * CHUNK : (chunk + 1) * CHUNK], result[:])
+        def finish(first, width, store_queue):
+            t_ps = second_layer(T_NET, w2t_sb, first, width, width)
+            scaled = products[first // CHUNK][:, first % CHUNK : first % CHUNK + width]
+            result = work.tile([P, width], F32, name="result")
+            nc.vector.scalar_tensor_tensor(result[:], t_ps[:], b2t_sb[:], scaled, ADD, ADD)
+            store_queue.dma_start(out[:, first : first + width], result[:])
 
 
         first_layer(S_NET, 0, HALF)
         first_layer(S_NET, HALF, HALF)
         first_layer(T_NET, 0, HALF)
 
-        products = [scaled_zb(chunk, second_layer(S_NET, w2s_sb, chunk, S_GROUP)) for chunk in range(CHUNKS)]
+        products = [
+            scaled_zb(chunk, second_layer(S_NET, w2s_sb, chunk * CHUNK, CHUNK, S_GROUP)) for chunk in range(CHUNKS)
+        ]
 
         for chunk in range(HALF // CHUNK, CHUNKS):
             first_layer(T_NET, chunk * CHUNK, CHUNK)
 
-        for chunk in range(CHUNKS):
-            finish(chunk, second_layer(T_NET, w2t_sb, chunk, CHUNK), products[chunk])
+        pieces = [(chunk * CHUNK, CHUNK) for chunk in range(CHUNKS - 1)]
+        pieces += [(N - CHUNK, CHUNK // 2), (N - CHUNK // 2, CHUNK // 2)]
+        for i, (first, width) in enumerate(pieces):
+            finish(first, width, nc.sync if i % 2 == 0 else nc.scalar)

@@ -24,7 +24,7 @@ def tile_affinecoupling_kernel(tc, table, w, b1, w2s, b2s, w2t, b2t, zb, offs, o
     nc = tc.nc
     with (
         tc.tile_pool(name="held", bufs=1) as held,
-        tc.tile_pool(name="work", bufs=CHUNKS + 1) as work,
+        tc.tile_pool(name="work", bufs=CHUNKS) as work,
         tc.psum_pool(name="psum", bufs=BANKS) as psum,
     ):
         zeros = held.tile([P, 1], F32, name="zeros")
@@ -108,7 +108,5 @@ def tile_affinecoupling_kernel(tc, table, w, b1, w2s, b2s, w2t, b2t, zb, offs, o
         for chunk in range(HALF // CHUNK, CHUNKS):
             first_layer(T_NET, chunk * CHUNK, CHUNK)
 
-        pieces = [(chunk * CHUNK, CHUNK) for chunk in range(CHUNKS - 1)]
-        pieces += [(N - CHUNK, CHUNK // 2), (N - CHUNK // 2, CHUNK // 2)]
-        for i, (first, width) in enumerate(pieces):
-            finish(first, width, nc.sync if i % 2 == 0 else nc.scalar)
+        for chunk in range(CHUNKS):
+            finish(chunk * CHUNK, CHUNK, nc.sync if chunk % 2 == 0 else nc.scalar)

@@ -14,6 +14,7 @@ S_NET, T_NET = 0, 1
 HALF = 512
 CHUNK = 256
 CHUNKS = N // CHUNK
+EARLY_CHUNKS = 1
 S_GROUP = 64
 BANKS = 8
 
@@ -58,13 +59,13 @@ def tile_affinecoupling_kernel(tc, table, w, b1, w2s, b2s, w2t, b2t, zb, offs, o
 
         hidden = [held.tile([P, N], BF16, name=f"hidden{block}") for block in range(BLOCKS)]
 
-        def first_layer(net, first, width):
+        def first_layer(net, first, width, scalar_alone=False):
             picked = table_sb[:].indirect(offsets[:, first // 16 : (first + width) // 16])
             for block in range(net * NET_BLOCKS, (net + 1) * NET_BLOCKS):
                 h_ps = psum.tile([P, width], F32, name="h_ps", tag="bank")
                 nc.tensor.matmul(h_ps[:], w_sb[:, block * P : (block + 1) * P], picked, start=True, stop=True)
                 h_sb = hidden[block][:, first : first + width]
-                if block % 2 == 0:
+                if scalar_alone or block % 2 == 0:
                     nc.scalar.activation(h_sb, h_ps[:], RELU, bias=b1_sb[:, block, :])
                 else:
                     nc.vector.tensor_scalar(h_sb, h_ps[:], b1_sb[:, block, :], 0.0, ADD, MAX)
@@ -89,12 +90,12 @@ def tile_affinecoupling_kernel(tc, table, w, b1, w2s, b2s, w2t, b2t, zb, offs, o
             nc.vector.tensor_tensor(scaled[:], scale[:], zb_sb[:, chunk * CHUNK : (chunk + 1) * CHUNK], MULT)
             return scaled
 
-        def finish(first, width, store_queue):
-            t_ps = second_layer(T_NET, w2t_sb, first, width, width)
-            scaled = products[first // CHUNK][:, first % CHUNK : first % CHUNK + width]
-            result = work.tile([P, width], F32, name="result")
-            nc.vector.scalar_tensor_tensor(result[:], t_ps[:], b2t_sb[:], scaled, ADD, ADD)
-            store_queue.dma_start(out[:, first : first + width], result[:])
+        def finish(chunk):
+            samples = slice(chunk * CHUNK, (chunk + 1) * CHUNK)
+            t_ps = second_layer(T_NET, w2t_sb, chunk * CHUNK, CHUNK, CHUNK)
+            result = work.tile([P, CHUNK], F32, name="result")
+            nc.vector.scalar_tensor_tensor(result[:], t_ps[:], b2t_sb[:], products[chunk][:], ADD, ADD)
+            nc.sync.dma_start(out[:, samples], result[:])
 
 
         first_layer(S_NET, 0, HALF)
@@ -104,9 +105,11 @@ def tile_affinecoupling_kernel(tc, table, w, b1, w2s, b2s, w2t, b2t, zb, offs, o
         products = [
             scaled_zb(chunk, second_layer(S_NET, w2s_sb, chunk * CHUNK, CHUNK, S_GROUP)) for chunk in range(CHUNKS)
         ]
+        for chunk in range(EARLY_CHUNKS):
+            finish(chunk)
 
-        for chunk in range(HALF // CHUNK, CHUNKS):
-            first_layer(T_NET, chunk * CHUNK, CHUNK)
+        first_layer(T_NET, HALF, CHUNK, scalar_alone=True)
+        first_layer(T_NET, HALF + CHUNK, CHUNK)
 
-        for chunk in range(CHUNKS):
-            finish(chunk * CHUNK, CHUNK, nc.sync if chunk % 2 == 0 else nc.scalar)
+        for chunk in range(EARLY_CHUNKS, CHUNKS):
+            finish(chunk)

@@ -15,6 +15,7 @@ HALF = 512
 CHUNK = 256
 CHUNKS = N // CHUNK
 EARLY_CHUNKS = 1
+NARROW = 128
 S_GROUP = 64
 BANKS = 8
 
@@ -109,7 +110,8 @@ def tile_affinecoupling_kernel(tc, table, w, b1, w2s, b2s, w2t, b2t, zb, offs, o
             finish(chunk)
 
         first_layer(T_NET, HALF, CHUNK, scalar_alone=True)
-        first_layer(T_NET, HALF + CHUNK, CHUNK)
+        for first in range(N - CHUNK, N, NARROW):
+            first_layer(T_NET, first, NARROW)
 
         for chunk in range(EARLY_CHUNKS, CHUNKS):
             finish(chunk)

@@ -37,11 +37,11 @@ def tile_affinecoupling_kernel(tc, table, w, b1, w2s, b2s, w2t, b2t, zb, offs, o
         offsets = held.tile([P, N // 16], U16, name="offsets")
         nc.sync.dma_start(offsets[:], offs)
         w_sb = held.tile([P, HIDDEN], BF16, name="w_sb")
-        nc.scalar.dma_start(w_sb[:, : HIDDEN // 2], w[:, : HIDDEN // 2])
+        nc.scalar.dma_start(w_sb[:, :P], w[:, :P])
 
         table_warm = held.tile([P, 1], F32, name="table_warm")
         nc.scalar.activation(table_warm[:], zeros[:], EXP)
-        nc.scalar.dma_start(w_sb[:, HIDDEN // 2 :], w[:, HIDDEN // 2 :])
+        nc.scalar.dma_start(w_sb[:, P:], w[:, P:])
 
         b1_sb = held.tile([P, BLOCKS, 1], F32, name="b1_sb")
         b2s_sb = held.tile([P, 1], F32, name="b2s_sb")
@@ -60,16 +60,17 @@ def tile_affinecoupling_kernel(tc, table, w, b1, w2s, b2s, w2t, b2t, zb, offs, o
 
         hidden = [held.tile([P, N], BF16, name=f"hidden{block}") for block in range(BLOCKS)]
 
-        def first_layer(net, first, width, scalar_alone=False):
-            picked = table_sb[:].indirect(offsets[:, first // 16 : (first + width) // 16])
+        def first_layer(net, first, last, width, scalar_alone=False):
             for block in range(net * NET_BLOCKS, (net + 1) * NET_BLOCKS):
-                h_ps = psum.tile([P, width], F32, name="h_ps", tag="bank")
-                nc.tensor.matmul(h_ps[:], w_sb[:, block * P : (block + 1) * P], picked, start=True, stop=True)
-                h_sb = hidden[block][:, first : first + width]
-                if scalar_alone or block % 2 == 0:
-                    nc.scalar.activation(h_sb, h_ps[:], RELU, bias=b1_sb[:, block, :])
-                else:
-                    nc.vector.tensor_scalar(h_sb, h_ps[:], b1_sb[:, block, :], 0.0, ADD, MAX)
+                for start in range(first, last, width):
+                    picked = table_sb[:].indirect(offsets[:, start // 16 : (start + width) // 16])
+                    h_ps = psum.tile([P, width], F32, name="h_ps", tag="bank")
+                    nc.tensor.matmul(h_ps[:], w_sb[:, block * P : (block + 1) * P], picked, start=True, stop=True)
+                    h_sb = hidden[block][:, start : start + width]
+                    if scalar_alone or block % 2 == 0:
+                        nc.scalar.activation(h_sb, h_ps[:], RELU, bias=b1_sb[:, block, :])
+                    else:
+                        nc.vector.tensor_scalar(h_sb, h_ps[:], b1_sb[:, block, :], 0.0, ADD, MAX)
 
         def second_layer(net, weights, first, width, group):
             net_ps = psum.tile([P, width], F32, name="net_ps", tag="bank")
@@ -99,9 +100,8 @@ def tile_affinecoupling_kernel(tc, table, w, b1, w2s, b2s, w2t, b2t, zb, offs, o
             nc.sync.dma_start(out[:, samples], result[:])
 
 
-        first_layer(S_NET, 0, HALF)
-        first_layer(S_NET, HALF, HALF)
-        first_layer(T_NET, 0, HALF)
+        first_layer(S_NET, 0, N, HALF)
+        first_layer(T_NET, 0, HALF, HALF)
 
         products = [
             scaled_zb(chunk, second_layer(S_NET, w2s_sb, chunk * CHUNK, CHUNK, S_GROUP)) for chunk in range(CHUNKS)
@@ -109,9 +109,9 @@ def tile_affinecoupling_kernel(tc, table, w, b1, w2s, b2s, w2t, b2t, zb, offs, o
         for chunk in range(EARLY_CHUNKS):
             finish(chunk)
 
-        first_layer(T_NET, HALF, CHUNK, scalar_alone=True)
-        for first in range(N - CHUNK, N, NARROW):
-            first_layer(T_NET, first, NARROW)
+        first_layer(T_NET, HALF, HALF + CHUNK, CHUNK, scalar_alone=True)
+        for first in range(HALF + CHUNK, N, NARROW):
+            first_layer(T_NET, first, first + NARROW, NARROW)
 
         for chunk in range(EARLY_CHUNKS, CHUNKS):
             finish(chunk)

import concourse.mybir as mybir

BF16, F32, U16 = mybir.dt.bfloat16, mybir.dt.float32, mybir.dt.uint16
ADD, MAX, MULT = mybir.AluOpType.add, mybir.AluOpType.max, mybir.AluOpType.mult
RELU, EXP = mybir.ActivationFunctionType.Relu, mybir.ActivationFunctionType.Exp

P = 128
STORE = 512
HIDDEN = 512
N = 1024
BLOCKS = HIDDEN // P
NET_BLOCKS = BLOCKS // 2
S_NET, T_NET = 0, 1
HALF = 512
CHUNK = 256
CHUNKS = N // CHUNK
EARLY_CHUNKS = 1
NARROW = 128
S_GROUP = 64
BANKS = 8

FLOPS = 2 * P * HIDDEN * N + 2 * HIDDEN * P * N


def tile_affinecoupling_kernel(tc, table, w, b1, w2s, b2s, w2t, b2t, zb, offs, out):
    nc = tc.nc
    with (
        tc.tile_pool(name="held", bufs=1) as held,
        tc.tile_pool(name="work", bufs=CHUNKS) as work,
        tc.psum_pool(name="psum", bufs=BANKS) as psum,
    ):
        zeros = held.tile([P, 1], F32, name="zeros")
        nc.vector.memset(zeros[:], 0.0)

        table_sb = held.tile([P, STORE], BF16, name="table_sb")
        nc.sync.dma_start(table_sb[:], table)
        offsets = held.tile([P, N // 16], U16, name="offsets")
        nc.sync.dma_start(offsets[:], offs)
        w_sb = held.tile([P, HIDDEN], BF16, name="w_sb")
        nc.scalar.dma_start(w_sb[:, :P], w[:, :P])

        table_warm = held.tile([P, 1], F32, name="table_warm")
        nc.scalar.activation(table_warm[:], zeros[:], EXP)
        nc.scalar.dma_start(w_sb[:, P:], w[:, P:])

        b1_sb = held.tile([P, BLOCKS, 1], F32, name="b1_sb")
        b2s_sb = held.tile([P, 1], F32, name="b2s_sb")
        b2t_sb = held.tile([P, 1], F32, name="b2t_sb")
        with nc.allow_non_contiguous_dma(reason="biases: one float32 a partition"):
            nc.sync.dma_start(b1_sb[:], b1.rearrange("(b p) o -> p b o", p=P))
            nc.sync.dma_start(b2s_sb[:], b2s)
            nc.sync.dma_start(b2t_sb[:], b2t)

        w2s_sb = held.tile([P, NET_BLOCKS, P], BF16, name="w2s_sb")
        nc.scalar.dma_start(w2s_sb[:], w2s.rearrange("(b p) c -> p b c", p=P))
        w2t_sb = held.tile([P, NET_BLOCKS, P], BF16, name="w2t_sb")
        nc.scalar.dma_start(w2t_sb[:], w2t.rearrange("(b p) c -> p b c", p=P))
        zb_sb = held.tile([P, N], F32, name="zb_sb")
        nc.sync.dma_start(zb_sb[:], zb)

        hidden = [held.tile([P, N], BF16, name=f"hidden{block}") for block in range(BLOCKS)]

        def first_layer(net, first, last, width, scalar_alone=False):
            for block in range(net * NET_BLOCKS, (net + 1) * NET_BLOCKS):
                for start in range(first, last, width):
                    picked = table_sb[:].indirect(offsets[:, start // 16 : (start + width) // 16])
                    h_ps = psum.tile([P, width], F32, name="h_ps", tag="bank")
                    nc.tensor.matmul(h_ps[:], w_sb[:, block * P : (block + 1) * P], picked, start=True, stop=True)
                    h_sb = hidden[block][:, start : start + width]
                    if scalar_alone or block % 2 == 0:
                        nc.scalar.activation(h_sb, h_ps[:], RELU, bias=b1_sb[:, block, :])
                    else:
                        nc.vector.tensor_scalar(h_sb, h_ps[:], b1_sb[:, block, :], 0.0, ADD, MAX)

        def second_layer(net, weights, first, width, group):
            net_ps = psum.tile([P, width], F32, name="net_ps", tag="bank")
            for col in range(0, width, group):
                for b in range(NET_BLOCKS):
                    nc.tensor.matmul(
                        net_ps[:, col : col + group],
                        weights[:, b, :],
                        hidden[net * NET_BLOCKS + b][:, first + col : first + col + group],
                        start=(b == 0),
                        stop=(b == NET_BLOCKS - 1),
                    )
            return net_ps

        def scaled_zb(chunk, s_ps):
            scale = work.tile([P, CHUNK], F32, name="scale")
            nc.scalar.activation(scale[:], s_ps[:], EXP, bias=b2s_sb[:])
            scaled = work.tile([P, CHUNK], F32, name="scaled")
            nc.vector.tensor_tensor(scaled[:], scale[:], zb_sb[:, chunk * CHUNK : (chunk + 1) * CHUNK], MULT)
            return scaled

        def finish(chunk):
            samples = slice(chunk * CHUNK, (chunk + 1) * CHUNK)
            t_ps = second_layer(T_NET, w2t_sb, chunk * CHUNK, CHUNK, CHUNK)
            result = work.tile([P, CHUNK], F32, name="result")
            nc.vector.scalar_tensor_tensor(result[:], t_ps[:], b2t_sb[:], products[chunk][:], ADD, ADD)
            nc.sync.dma_start(out[:, samples], result[:])


        first_layer(S_NET, 0, N, HALF)
        first_layer(T_NET, 0, HALF, HALF)

        products = [
            scaled_zb(chunk, second_layer(S_NET, w2s_sb, chunk * CHUNK, CHUNK, S_GROUP)) for chunk in range(CHUNKS)
        ]
        for chunk in range(EARLY_CHUNKS):
            finish(chunk)

        first_layer(T_NET, HALF, HALF + CHUNK, CHUNK, scalar_alone=True)
        for first in range(HALF + CHUNK, N, NARROW):
            first_layer(T_NET, first, first + NARROW, NARROW)

        for chunk in range(EARLY_CHUNKS, CHUNKS):
            finish(chunk)
